import numpy as np
import ml_dtypes

BF16 = ml_dtypes.bfloat16


def bf(x):
    return np.asarray(x, np.float32).astype(BF16)


def f32(x):
    return np.asarray(x, np.float32)


def f64(x):
    return np.asarray(x).astype(np.float64)


def striped(idx):
    return np.tile(idx.reshape(-1, 16).T, (8, 1))


C, S, N, H = 128, 256, 512, 128
WB = 0.5


def setup_inputs():
    return {"left": f32(np.random.standard_normal((C, S))), "right": f32(np.random.standard_normal((C, N))), "w": f32(np.random.uniform(-WB, WB, (C, H))), "offs": striped(np.random.permutation(np.tile(np.arange(S), 2))[:N])}


def reference(left, right, w, offs):
    idx = offs[:16].T.reshape(-1)
    lg = f64(left)[:, idx]
    w2 = f64(w) ** 2
    dot = w2.T @ (lg * f64(right))
    nl = np.sqrt(w2.T @ (lg * lg))
    return dot / nl

@@ -1,0 +1,58 @@
+import concourse.mybir as mybir
+
+C, S, N, H = 128, 256, 512, 128
+PIECE = S
+PIECES = N // PIECE
+COLS = PIECE // 16
+
+FLOPS = 2 * (2 * C * H * N)
+
+F32, BF16, U16 = mybir.dt.float32, mybir.dt.bfloat16, mybir.dt.uint16
+MULT = mybir.AluOpType.mult
+FUNC = mybir.ActivationFunctionType
+
+
+def tile_graphgenerator_kernel(tc, left, right, w, offs, out):
+    nc = tc.nc
+    with (
+        tc.tile_pool(name="held", bufs=1) as held,
+        tc.psum_pool(name="psum", bufs=1) as psum,
+    ):
+        offsets = held.tile([C, N // 16], U16, name="offsets")
+        nc.sync.dma_start(offsets[:], offs)
+        left_f32 = held.tile([C, S], F32, name="left_f32")
+        nc.sync.dma_start(left_f32[:], left)
+        w_f32 = held.tile([C, H], F32, name="w_f32")
+        nc.scalar.dma_start(w_f32[:], w)
+        right_f32 = [held.tile([C, PIECE], F32, name=f"right_f32_{p}") for p in range(PIECES)]
+        nc.scalar.dma_start(right_f32[0][:], right[:, 0:PIECE])
+        nc.sync.dma_start(right_f32[1][:], right[:, PIECE : 2 * PIECE])
+
+        w_sq = held.tile([C, H], BF16, name="w_sq")
+        nc.scalar.activation(w_sq[:], w_f32[:], FUNC.Square)
+
+        nl_sq = [psum.tile([H, PIECE], F32, name=f"nl_sq_{p}") for p in range(PIECES)]
+        dot = [psum.tile([H, PIECE], F32, name=f"dot_{p}") for p in range(PIECES)]
+        inv_nl = [held.tile([H, PIECE], F32, name=f"inv_nl_{p}") for p in range(PIECES)]
+        for p in range(PIECES):
+            piece_offsets = offsets[:, p * COLS : (p + 1) * COLS]
+
+            picked = held.tile([C, PIECE], F32, name=f"picked_{p}")
+            nc.vector.tensor_copy(picked[:], left_f32[:].indirect(piece_offsets))
+            picked_sq = held.tile([C, PIECE], BF16, name=f"picked_sq_{p}")
+            nc.scalar.activation(picked_sq[:], picked[:], FUNC.Square)
+            nc.tensor.matmul(nl_sq[p][:], w_sq[:], picked_sq[:], start=True, stop=True)
+
+            prod_f32 = held.tile([C, PIECE], F32, name=f"prod_f32_{p}")
+            nc.vector.tensor_tensor(prod_f32[:], left_f32[:].indirect(piece_offsets), right_f32[p][:], MULT)
+            prod = held.tile([C, PIECE], BF16, name=f"prod_{p}")
+            nc.scalar.activation(prod[:], prod_f32[:], FUNC.Copy)
+            nc.tensor.matmul(dot[p][:], w_sq[:], prod[:], start=True, stop=True)
+
+            nc.scalar.activation(inv_nl[p][:], nl_sq[p][:], FUNC.Abs_reciprocal_sqrt)
+
+        for p in range(PIECES):
+            score = held.tile([H, PIECE], F32, name=f"score_{p}")
+            nc.vector.tensor_tensor(score[:], dot[p][:], inv_nl[p][:], MULT)
+            store_queue = nc.sync if p % 2 == 0 else nc.scalar
+            store_queue.dma_start(out[:, p * PIECE : (p + 1) * PIECE], score[:])

@@ -25,31 +25,31 @@ def tile_graphgenerator_kernel(tc, left, right, w, offs, out):
         w_f32 = held.tile([C, H], F32, name="w_f32")
         nc.scalar.dma_start(w_f32[:], w)
         right_f32 = [held.tile([C, PIECE], F32, name=f"right_f32_{p}") for p in range(PIECES)]
-        nc.scalar.dma_start(right_f32[0][:], right[:, 0:PIECE])
-        nc.sync.dma_start(right_f32[1][:], right[:, PIECE : 2 * PIECE])
+        for p in range(PIECES):
+            nc.sync.dma_start(right_f32[p][:], right[:, p * PIECE : (p + 1) * PIECE])
+
+        piece_offsets = [offsets[:, p * COLS : (p + 1) * COLS] for p in range(PIECES)]
 
         w_sq = held.tile([C, H], BF16, name="w_sq")
         nc.scalar.activation(w_sq[:], w_f32[:], FUNC.Square)
 
-        nl_sq = [psum.tile([H, PIECE], F32, name=f"nl_sq_{p}") for p in range(PIECES)]
-        dot = [psum.tile([H, PIECE], F32, name=f"dot_{p}") for p in range(PIECES)]
         inv_nl = [held.tile([H, PIECE], F32, name=f"inv_nl_{p}") for p in range(PIECES)]
         for p in range(PIECES):
-            piece_offsets = offsets[:, p * COLS : (p + 1) * COLS]
-
             picked = held.tile([C, PIECE], F32, name=f"picked_{p}")
-            nc.vector.tensor_copy(picked[:], left_f32[:].indirect(piece_offsets))
+            nc.vector.tensor_copy(picked[:], left_f32[:].indirect(piece_offsets[p]))
             picked_sq = held.tile([C, PIECE], BF16, name=f"picked_sq_{p}")
             nc.scalar.activation(picked_sq[:], picked[:], FUNC.Square)
-            nc.tensor.matmul(nl_sq[p][:], w_sq[:], picked_sq[:], start=True, stop=True)
+            nl_sq = psum.tile([H, PIECE], F32, name=f"nl_sq_{p}")
+            nc.tensor.matmul(nl_sq[:], w_sq[:], picked_sq[:], start=True, stop=True)
+            nc.scalar.activation(inv_nl[p][:], nl_sq[:], FUNC.Abs_reciprocal_sqrt)
 
+        dot = [psum.tile([H, PIECE], F32, name=f"dot_{p}") for p in range(PIECES)]
+        for p in range(PIECES):
             prod_f32 = held.tile([C, PIECE], F32, name=f"prod_f32_{p}")
-            nc.vector.tensor_tensor(prod_f32[:], left_f32[:].indirect(piece_offsets), right_f32[p][:], MULT)
+            nc.vector.tensor_tensor(prod_f32[:], left_f32[:].indirect(piece_offsets[p]), right_f32[p][:], MULT)
             prod = held.tile([C, PIECE], BF16, name=f"prod_{p}")
-            nc.scalar.activation(prod[:], prod_f32[:], FUNC.Copy)
+            nc.vector.tensor_copy(prod[:], prod_f32[:])
             nc.tensor.matmul(dot[p][:], w_sq[:], prod[:], start=True, stop=True)
-
-            nc.scalar.activation(inv_nl[p][:], nl_sq[p][:], FUNC.Abs_reciprocal_sqrt)
 
         for p in range(PIECES):
             score = held.tile([H, PIECE], F32, name=f"score_{p}")

@@ -28,28 +28,36 @@ def tile_graphgenerator_kernel(tc, left, right, w, offs, out):
         for p in range(PIECES):
             nc.sync.dma_start(right_f32[p][:], right[:, p * PIECE : (p + 1) * PIECE])
 
+        scratch = held.tile([C, 1], F32, name="scratch")
+        nc.gpsimd.memset(scratch[:], 1.0)
+        warmed = held.tile([C, 1], F32, name="warmed")
+        nc.scalar.activation(warmed[:], scratch[:], FUNC.Abs_reciprocal_sqrt)
+
         piece_offsets = [offsets[:, p * COLS : (p + 1) * COLS] for p in range(PIECES)]
 
         w_sq = held.tile([C, H], BF16, name="w_sq")
         nc.scalar.activation(w_sq[:], w_f32[:], FUNC.Square)
 
-        inv_nl = [held.tile([H, PIECE], F32, name=f"inv_nl_{p}") for p in range(PIECES)]
+        nl_sq = [psum.tile([H, PIECE], F32, name=f"nl_sq_{p}") for p in range(PIECES)]
         for p in range(PIECES):
             picked = held.tile([C, PIECE], F32, name=f"picked_{p}")
             nc.vector.tensor_copy(picked[:], left_f32[:].indirect(piece_offsets[p]))
             picked_sq = held.tile([C, PIECE], BF16, name=f"picked_sq_{p}")
             nc.scalar.activation(picked_sq[:], picked[:], FUNC.Square)
-            nl_sq = psum.tile([H, PIECE], F32, name=f"nl_sq_{p}")
-            nc.tensor.matmul(nl_sq[:], w_sq[:], picked_sq[:], start=True, stop=True)
-            nc.scalar.activation(inv_nl[p][:], nl_sq[:], FUNC.Abs_reciprocal_sqrt)
+            nc.tensor.matmul(nl_sq[p][:], w_sq[:], picked_sq[:], start=True, stop=True)
 
         dot = [psum.tile([H, PIECE], F32, name=f"dot_{p}") for p in range(PIECES)]
+        inv_nl = [held.tile([H, PIECE], F32, name=f"inv_nl_{p}") for p in range(PIECES)]
         for p in range(PIECES):
             prod_f32 = held.tile([C, PIECE], F32, name=f"prod_f32_{p}")
             nc.vector.tensor_tensor(prod_f32[:], left_f32[:].indirect(piece_offsets[p]), right_f32[p][:], MULT)
             prod = held.tile([C, PIECE], BF16, name=f"prod_{p}")
-            nc.vector.tensor_copy(prod[:], prod_f32[:])
+            if p < PIECES - 1:
+                nc.scalar.activation(prod[:], prod_f32[:], FUNC.Copy)
+            else:
+                nc.vector.tensor_copy(prod[:], prod_f32[:])
             nc.tensor.matmul(dot[p][:], w_sq[:], prod[:], start=True, stop=True)
+            nc.scalar.activation(inv_nl[p][:], nl_sq[p][:], FUNC.Abs_reciprocal_sqrt)
 
         for p in range(PIECES):
             score = held.tile([H, PIECE], F32, name=f"score_{p}")

@@ -21,7 +21,7 @@ def tile_graphgenerator_kernel(tc, left, right, w, offs, out):
         offsets = held.tile([C, N // 16], U16, name="offsets")
         nc.sync.dma_start(offsets[:], offs)
         left_f32 = held.tile([C, S], F32, name="left_f32")
-        nc.sync.dma_start(left_f32[:], left)
+        nc.scalar.dma_start(left_f32[:], left)
         w_f32 = held.tile([C, H], F32, name="w_f32")
         nc.scalar.dma_start(w_f32[:], w)
         right_f32 = [held.tile([C, PIECE], F32, name=f"right_f32_{p}") for p in range(PIECES)]
@@ -62,5 +62,5 @@ def tile_graphgenerator_kernel(tc, left, right, w, offs, out):
         for p in range(PIECES):
             score = held.tile([H, PIECE], F32, name=f"score_{p}")
             nc.vector.tensor_tensor(score[:], dot[p][:], inv_nl[p][:], MULT)
-            store_queue = nc.sync if p % 2 == 0 else nc.scalar
+            store_queue = nc.scalar if p % 2 == 0 else nc.sync
             store_queue.dma_start(out[:, p * PIECE : (p + 1) * PIECE], score[:])

@@ -23,10 +23,11 @@ def tile_graphgenerator_kernel(tc, left, right, w, offs, out):
         left_f32 = held.tile([C, S], F32, name="left_f32")
         nc.scalar.dma_start(left_f32[:], left)
         w_f32 = held.tile([C, H], F32, name="w_f32")
-        nc.scalar.dma_start(w_f32[:], w)
+        nc.sync.dma_start(w_f32[:], w)
         right_f32 = [held.tile([C, PIECE], F32, name=f"right_f32_{p}") for p in range(PIECES)]
         for p in range(PIECES):
-            nc.sync.dma_start(right_f32[p][:], right[:, p * PIECE : (p + 1) * PIECE])
+            load_queue = nc.scalar if p % 2 == 0 else nc.sync
+            load_queue.dma_start(right_f32[p][:], right[:, p * PIECE : (p + 1) * PIECE])
 
         scratch = held.tile([C, 1], F32, name="scratch")
         nc.gpsimd.memset(scratch[:], 1.0)

@@ -23,11 +23,10 @@ def tile_graphgenerator_kernel(tc, left, right, w, offs, out):
         left_f32 = held.tile([C, S], F32, name="left_f32")
         nc.scalar.dma_start(left_f32[:], left)
         w_f32 = held.tile([C, H], F32, name="w_f32")
-        nc.sync.dma_start(w_f32[:], w)
+        nc.scalar.dma_start(w_f32[:], w)
         right_f32 = [held.tile([C, PIECE], F32, name=f"right_f32_{p}") for p in range(PIECES)]
         for p in range(PIECES):
-            load_queue = nc.scalar if p % 2 == 0 else nc.sync
-            load_queue.dma_start(right_f32[p][:], right[:, p * PIECE : (p + 1) * PIECE])
+            nc.sync.dma_start(right_f32[p][:], right[:, p * PIECE : (p + 1) * PIECE])
 
         scratch = held.tile([C, 1], F32, name="scratch")
         nc.gpsimd.memset(scratch[:], 1.0)
@@ -63,5 +62,5 @@ def tile_graphgenerator_kernel(tc, left, right, w, offs, out):
         for p in range(PIECES):
             score = held.tile([H, PIECE], F32, name=f"score_{p}")
             nc.vector.tensor_tensor(score[:], dot[p][:], inv_nl[p][:], MULT)
-            store_queue = nc.scalar if p % 2 == 0 else nc.sync
+            store_queue = nc.sync if p % 2 == 0 else nc.scalar
             store_queue.dma_start(out[:, p * PIECE : (p + 1) * PIECE], score[:])

@@ -35,29 +35,28 @@ def tile_graphgenerator_kernel(tc, left, right, w, offs, out):
 
         piece_offsets = [offsets[:, p * COLS : (p + 1) * COLS] for p in range(PIECES)]
 
+        left_sq = held.tile([C, S], BF16, name="left_sq")
+        nc.scalar.activation(left_sq[:], left_f32[:], FUNC.Square)
         w_sq = held.tile([C, H], BF16, name="w_sq")
         nc.scalar.activation(w_sq[:], w_f32[:], FUNC.Square)
+        node_nl_sq = psum.tile([H, S], F32, name="node_nl_sq")
+        nc.tensor.matmul(node_nl_sq[:], w_sq[:], left_sq[:], start=True, stop=True)
+        node_inv_nl = held.tile([H, S], F32, name="node_inv_nl")
+        nc.scalar.activation(node_inv_nl[:], node_nl_sq[:], FUNC.Abs_reciprocal_sqrt)
 
-        nl_sq = [psum.tile([H, PIECE], F32, name=f"nl_sq_{p}") for p in range(PIECES)]
+        prod_f32 = [held.tile([C, PIECE], F32, name=f"prod_f32_{p}") for p in range(PIECES)]
         for p in range(PIECES):
-            picked = held.tile([C, PIECE], F32, name=f"picked_{p}")
-            nc.vector.tensor_copy(picked[:], left_f32[:].indirect(piece_offsets[p]))
-            picked_sq = held.tile([C, PIECE], BF16, name=f"picked_sq_{p}")
-            nc.scalar.activation(picked_sq[:], picked[:], FUNC.Square)
-            nc.tensor.matmul(nl_sq[p][:], w_sq[:], picked_sq[:], start=True, stop=True)
+            nc.vector.tensor_tensor(prod_f32[p][:], left_f32[:].indirect(piece_offsets[p]), right_f32[p][:], MULT)
 
         dot = [psum.tile([H, PIECE], F32, name=f"dot_{p}") for p in range(PIECES)]
+        for p in range(PIECES):
+            prod = held.tile([C, PIECE], BF16, name=f"prod_{p}")
+            nc.vector.tensor_copy(prod[:], prod_f32[p][:])
+            nc.tensor.matmul(dot[p][:], w_sq[:], prod[:], start=True, stop=True)
+
         inv_nl = [held.tile([H, PIECE], F32, name=f"inv_nl_{p}") for p in range(PIECES)]
         for p in range(PIECES):
-            prod_f32 = held.tile([C, PIECE], F32, name=f"prod_f32_{p}")
-            nc.vector.tensor_tensor(prod_f32[:], left_f32[:].indirect(piece_offsets[p]), right_f32[p][:], MULT)
-            prod = held.tile([C, PIECE], BF16, name=f"prod_{p}")
-            if p < PIECES - 1:
-                nc.scalar.activation(prod[:], prod_f32[:], FUNC.Copy)
-            else:
-                nc.vector.tensor_copy(prod[:], prod_f32[:])
-            nc.tensor.matmul(dot[p][:], w_sq[:], prod[:], start=True, stop=True)
-            nc.scalar.activation(inv_nl[p][:], nl_sq[p][:], FUNC.Abs_reciprocal_sqrt)
+            nc.vector.tensor_copy(inv_nl[p][:], node_inv_nl[:].indirect(piece_offsets[p]))
 
         for p in range(PIECES):
             score = held.tile([H, PIECE], F32, name=f"score_{p}")

@@ -35,14 +35,25 @@ def tile_graphgenerator_kernel(tc, left, right, w, offs, out):
 
         piece_offsets = [offsets[:, p * COLS : (p + 1) * COLS] for p in range(PIECES)]
 
+        picked = held.tile([C, PIECE], F32, name="picked")
+        nc.vector.tensor_copy(picked[:], left_f32[:].indirect(piece_offsets[0]))
+
         left_sq = held.tile([C, S], BF16, name="left_sq")
         nc.scalar.activation(left_sq[:], left_f32[:], FUNC.Square)
         w_sq = held.tile([C, H], BF16, name="w_sq")
         nc.scalar.activation(w_sq[:], w_f32[:], FUNC.Square)
         node_nl_sq = psum.tile([H, S], F32, name="node_nl_sq")
         nc.tensor.matmul(node_nl_sq[:], w_sq[:], left_sq[:], start=True, stop=True)
+
+        picked_sq = held.tile([C, PIECE], BF16, name="picked_sq")
+        nc.scalar.activation(picked_sq[:], picked[:], FUNC.Square)
+        nl_sq = psum.tile([H, PIECE], F32, name="nl_sq")
+        nc.tensor.matmul(nl_sq[:], w_sq[:], picked_sq[:], start=True, stop=True)
+
+        inv_nl = [held.tile([H, PIECE], F32, name=f"inv_nl_{p}") for p in range(PIECES)]
         node_inv_nl = held.tile([H, S], F32, name="node_inv_nl")
         nc.scalar.activation(node_inv_nl[:], node_nl_sq[:], FUNC.Abs_reciprocal_sqrt)
+        nc.scalar.activation(inv_nl[0][:], nl_sq[:], FUNC.Abs_reciprocal_sqrt)
 
         prod_f32 = [held.tile([C, PIECE], F32, name=f"prod_f32_{p}") for p in range(PIECES)]
         for p in range(PIECES):
@@ -54,9 +65,7 @@ def tile_graphgenerator_kernel(tc, left, right, w, offs, out):
             nc.vector.tensor_copy(prod[:], prod_f32[p][:])
             nc.tensor.matmul(dot[p][:], w_sq[:], prod[:], start=True, stop=True)
 
-        inv_nl = [held.tile([H, PIECE], F32, name=f"inv_nl_{p}") for p in range(PIECES)]
-        for p in range(PIECES):
-            nc.vector.tensor_copy(inv_nl[p][:], node_inv_nl[:].indirect(piece_offsets[p]))
+        nc.vector.tensor_copy(inv_nl[1][:], node_inv_nl[:].indirect(piece_offsets[1]))
 
         for p in range(PIECES):
             score = held.tile([H, PIECE], F32, name=f"score_{p}")

@@ -41,7 +41,7 @@ def tile_graphgenerator_kernel(tc, left, right, w, offs, out):
         left_sq = held.tile([C, S], BF16, name="left_sq")
         nc.scalar.activation(left_sq[:], left_f32[:], FUNC.Square)
         w_sq = held.tile([C, H], BF16, name="w_sq")
-        nc.scalar.activation(w_sq[:], w_f32[:], FUNC.Square)
+        nc.vector.tensor_tensor(w_sq[:], w_f32[:], w_f32[:], MULT)
         node_nl_sq = psum.tile([H, S], F32, name="node_nl_sq")
         nc.tensor.matmul(node_nl_sq[:], w_sq[:], left_sq[:], start=True, stop=True)
 

@@ -70,5 +70,4 @@ def tile_graphgenerator_kernel(tc, left, right, w, offs, out):
         for p in range(PIECES):
             score = held.tile([H, PIECE], F32, name=f"score_{p}")
             nc.vector.tensor_tensor(score[:], dot[p][:], inv_nl[p][:], MULT)
-            store_queue = nc.sync if p % 2 == 0 else nc.scalar
-            store_queue.dma_start(out[:, p * PIECE : (p + 1) * PIECE], score[:])
+            nc.scalar.dma_start(out[:, p * PIECE : (p + 1) * PIECE], score[:])

@@ -55,15 +55,19 @@ def tile_graphgenerator_kernel(tc, left, right, w, offs, out):
         nc.scalar.activation(node_inv_nl[:], node_nl_sq[:], FUNC.Abs_reciprocal_sqrt)
         nc.scalar.activation(inv_nl[0][:], nl_sq[:], FUNC.Abs_reciprocal_sqrt)
 
-        prod_f32 = [held.tile([C, PIECE], F32, name=f"prod_f32_{p}") for p in range(PIECES)]
-        for p in range(PIECES):
-            nc.vector.tensor_tensor(prod_f32[p][:], left_f32[:].indirect(piece_offsets[p]), right_f32[p][:], MULT)
+        cuts = [(0, 0, PIECE), (1, 0, PIECE // 2), (1, PIECE // 2, PIECE // 2)]
+        prod_f32 = [held.tile([C, width], F32, name=f"prod_f32_{i}") for i, (p, first, width) in enumerate(cuts)]
+        for i, (p, first, width) in enumerate(cuts):
+            cut_offsets = offsets[:, (p * PIECE + first) // 16 : (p * PIECE + first + width) // 16]
+            nc.vector.tensor_tensor(
+                prod_f32[i][:], left_f32[:].indirect(cut_offsets), right_f32[p][:, first : first + width], MULT
+            )
 
         dot = [psum.tile([H, PIECE], F32, name=f"dot_{p}") for p in range(PIECES)]
-        for p in range(PIECES):
-            prod = held.tile([C, PIECE], BF16, name=f"prod_{p}")
-            nc.vector.tensor_copy(prod[:], prod_f32[p][:])
-            nc.tensor.matmul(dot[p][:], w_sq[:], prod[:], start=True, stop=True)
+        for i, (p, first, width) in enumerate(cuts):
+            prod = held.tile([C, width], BF16, name=f"prod_{i}")
+            nc.vector.tensor_copy(prod[:], prod_f32[i][:])
+            nc.tensor.matmul(dot[p][:, first : first + width], w_sq[:], prod[:], start=True, stop=True)
 
         nc.vector.tensor_copy(inv_nl[1][:], node_inv_nl[:].indirect(piece_offsets[1]))
 

@@ -57,17 +57,22 @@ def tile_graphgenerator_kernel(tc, left, right, w, offs, out):
 
         cuts = [(0, 0, PIECE), (1, 0, PIECE // 2), (1, PIECE // 2, PIECE // 2)]
         prod_f32 = [held.tile([C, width], F32, name=f"prod_f32_{i}") for i, (p, first, width) in enumerate(cuts)]
-        for i, (p, first, width) in enumerate(cuts):
-            cut_offsets = offsets[:, (p * PIECE + first) // 16 : (p * PIECE + first + width) // 16]
-            nc.vector.tensor_tensor(
-                prod_f32[i][:], left_f32[:].indirect(cut_offsets), right_f32[p][:, first : first + width], MULT
-            )
-
         dot = [psum.tile([H, PIECE], F32, name=f"dot_{p}") for p in range(PIECES)]
-        for i, (p, first, width) in enumerate(cuts):
-            prod = held.tile([C, width], BF16, name=f"prod_{i}")
-            nc.vector.tensor_copy(prod[:], prod_f32[i][:])
-            nc.tensor.matmul(dot[p][:, first : first + width], w_sq[:], prod[:], start=True, stop=True)
+        for i in range(len(cuts) + 1):
+            if i < len(cuts):
+                p, first, width = cuts[i]
+                cut_offsets = offsets[:, (p * PIECE + first) // 16 : (p * PIECE + first + width) // 16]
+                nc.vector.tensor_tensor(
+                    prod_f32[i][:], left_f32[:].indirect(cut_offsets), right_f32[p][:, first : first + width], MULT
+                )
+            if i > 0:
+                p, first, width = cuts[i - 1]
+                prod = held.tile([C, width], BF16, name=f"prod_{i - 1}")
+                if p == 0:
+                    nc.vector.tensor_copy(prod[:], prod_f32[i - 1][:])
+                else:
+                    nc.scalar.copy(prod[:], prod_f32[i - 1][:])
+                nc.tensor.matmul(dot[p][:, first : first + width], w_sq[:], prod[:], start=True, stop=True)
 
         nc.vector.tensor_copy(inv_nl[1][:], node_inv_nl[:].indirect(piece_offsets[1]))
 

@@ -57,7 +57,7 @@ def tile_graphgenerator_kernel(tc, left, right, w, offs, out):
 
         cuts = [(0, 0, PIECE), (1, 0, PIECE // 2), (1, PIECE // 2, PIECE // 2)]
         prod_f32 = [held.tile([C, width], F32, name=f"prod_f32_{i}") for i, (p, first, width) in enumerate(cuts)]
-        dot = [psum.tile([H, PIECE], F32, name=f"dot_{p}") for p in range(PIECES)]
+        dot = [psum.tile([H, width], F32, name=f"dot_{i}") for i, (p, first, width) in enumerate(cuts)]
         for i in range(len(cuts) + 1):
             if i < len(cuts):
                 p, first, width = cuts[i]
@@ -72,11 +72,13 @@ def tile_graphgenerator_kernel(tc, left, right, w, offs, out):
                     nc.vector.tensor_copy(prod[:], prod_f32[i - 1][:])
                 else:
                     nc.scalar.copy(prod[:], prod_f32[i - 1][:])
-                nc.tensor.matmul(dot[p][:, first : first + width], w_sq[:], prod[:], start=True, stop=True)
+                nc.tensor.matmul(dot[i - 1][:], w_sq[:], prod[:], start=True, stop=True)
 
         nc.vector.tensor_copy(inv_nl[1][:], node_inv_nl[:].indirect(piece_offsets[1]))
 
+        score = [held.tile([H, PIECE], F32, name=f"score_{p}") for p in range(PIECES)]
+        for i, (p, first, width) in enumerate(cuts):
+            cols = slice(first, first + width)
+            nc.vector.tensor_tensor(score[p][:, cols], dot[i][:], inv_nl[p][:, cols], MULT)
         for p in range(PIECES):
-            score = held.tile([H, PIECE], F32, name=f"score_{p}")
-            nc.vector.tensor_tensor(score[:], dot[p][:], inv_nl[p][:], MULT)
-            nc.scalar.dma_start(out[:, p * PIECE : (p + 1) * PIECE], score[:])
+            nc.scalar.dma_start(out[:, p * PIECE : (p + 1) * PIECE], score[p][:])

import concourse.mybir as mybir

C, S, N, H = 128, 256, 512, 128
PIECE = S
PIECES = N // PIECE
COLS = PIECE // 16

FLOPS = 2 * (2 * C * H * N)

F32, BF16, U16 = mybir.dt.float32, mybir.dt.bfloat16, mybir.dt.uint16
MULT = mybir.AluOpType.mult
FUNC = mybir.ActivationFunctionType


def tile_graphgenerator_kernel(tc, left, right, w, offs, out):
    nc = tc.nc
    with (
        tc.tile_pool(name="held", bufs=1) as held,
        tc.psum_pool(name="psum", bufs=1) as psum,
    ):
        offsets = held.tile([C, N // 16], U16, name="offsets")
        nc.sync.dma_start(offsets[:], offs)
        left_f32 = held.tile([C, S], F32, name="left_f32")
        nc.scalar.dma_start(left_f32[:], left)
        w_f32 = held.tile([C, H], F32, name="w_f32")
        nc.scalar.dma_start(w_f32[:], w)
        right_f32 = [held.tile([C, PIECE], F32, name=f"right_f32_{p}") for p in range(PIECES)]
        for p in range(PIECES):
            nc.sync.dma_start(right_f32[p][:], right[:, p * PIECE : (p + 1) * PIECE])

        scratch = held.tile([C, 1], F32, name="scratch")
        nc.gpsimd.memset(scratch[:], 1.0)
        warmed = held.tile([C, 1], F32, name="warmed")
        nc.scalar.activation(warmed[:], scratch[:], FUNC.Abs_reciprocal_sqrt)

        piece_offsets = [offsets[:, p * COLS : (p + 1) * COLS] for p in range(PIECES)]

        picked = held.tile([C, PIECE], F32, name="picked")
        nc.vector.tensor_copy(picked[:], left_f32[:].indirect(piece_offsets[0]))

        left_sq = held.tile([C, S], BF16, name="left_sq")
        nc.scalar.activation(left_sq[:], left_f32[:], FUNC.Square)
        w_sq = held.tile([C, H], BF16, name="w_sq")
        nc.vector.tensor_tensor(w_sq[:], w_f32[:], w_f32[:], MULT)
        node_nl_sq = psum.tile([H, S], F32, name="node_nl_sq")
        nc.tensor.matmul(node_nl_sq[:], w_sq[:], left_sq[:], start=True, stop=True)

        picked_sq = held.tile([C, PIECE], BF16, name="picked_sq")
        nc.scalar.activation(picked_sq[:], picked[:], FUNC.Square)
        nl_sq = psum.tile([H, PIECE], F32, name="nl_sq")
        nc.tensor.matmul(nl_sq[:], w_sq[:], picked_sq[:], start=True, stop=True)

        inv_nl = [held.tile([H, PIECE], F32, name=f"inv_nl_{p}") for p in range(PIECES)]
        node_inv_nl = held.tile([H, S], F32, name="node_inv_nl")
        nc.scalar.activation(node_inv_nl[:], node_nl_sq[:], FUNC.Abs_reciprocal_sqrt)
        nc.scalar.activation(inv_nl[0][:], nl_sq[:], FUNC.Abs_reciprocal_sqrt)

        cuts = [(0, 0, PIECE), (1, 0, PIECE // 2), (1, PIECE // 2, PIECE // 2)]
        prod_f32 = [held.tile([C, width], F32, name=f"prod_f32_{i}") for i, (p, first, width) in enumerate(cuts)]
        dot = [psum.tile([H, width], F32, name=f"dot_{i}") for i, (p, first, width) in enumerate(cuts)]
        for i in range(len(cuts) + 1):
            if i < len(cuts):
                p, first, width = cuts[i]
                cut_offsets = offsets[:, (p * PIECE + first) // 16 : (p * PIECE + first + width) // 16]
                nc.vector.tensor_tensor(
                    prod_f32[i][:], left_f32[:].indirect(cut_offsets), right_f32[p][:, first : first + width], MULT
                )
            if i > 0:
                p, first, width = cuts[i - 1]
                prod = held.tile([C, width], BF16, name=f"prod_{i - 1}")
                if p == 0:
                    nc.vector.tensor_copy(prod[:], prod_f32[i - 1][:])
                else:
                    nc.scalar.copy(prod[:], prod_f32[i - 1][:])
                nc.tensor.matmul(dot[i - 1][:], w_sq[:], prod[:], start=True, stop=True)

        nc.vector.tensor_copy(inv_nl[1][:], node_inv_nl[:].indirect(piece_offsets[1]))

        score = [held.tile([H, PIECE], F32, name=f"score_{p}") for p in range(PIECES)]
        for i, (p, first, width) in enumerate(cuts):
            cols = slice(first, first + width)
            nc.vector.tensor_tensor(score[p][:, cols], dot[i][:], inv_nl[p][:, cols], MULT)
        for p in range(PIECES):
            nc.scalar.dma_start(out[:, p * PIECE : (p + 1) * PIECE], score[p][:])
